import numpy as np
import ml_dtypes


def mxq(x, axis, fmt="e4m3"):
    dtype, down = {"e4m3": (ml_dtypes.float8_e4m3fn, 7), "e5m2": (ml_dtypes.float8_e5m2, 14)}[fmt]
    v = np.moveaxis(np.asarray(x, np.float32).astype(ml_dtypes.bfloat16).astype(np.float64), axis, -1)
    blocks = v.reshape(v.shape[:-1] + (-1, 32))
    amax = np.abs(blocks).max(-1, keepdims=True)
    byte = np.maximum(np.where(amax > 0, np.frexp(amax)[1] - 1 + 127, 0) - down, 1)
    scale = np.exp2(byte - 127.0)
    codes = (blocks / scale).astype(np.float32).astype(dtype).astype(np.float64)
    return np.moveaxis((codes * scale).reshape(v.shape), -1, axis)


WIDE = False


def mx_kscale(k):
    if not WIDE:
        return np.ones(k)
    levels = np.array([10, -10, 5, -5, 0])
    if k % 512:
        return np.exp2(np.random.permutation(np.resize(levels, k // 32))).repeat(32)
    a = np.empty((k // 512, 16))
    for p in range(k // 512):
        a[p, :8] = np.random.permutation(np.resize(levels, 8))
        for g in range(8):
            far = levels[np.abs(levels - a[p, g]) >= 10]
            a[p, g + 8] = far[np.random.randint(len(far))]
    return np.exp2(a.ravel()).repeat(32)


BF16 = ml_dtypes.bfloat16


def bf(x):
    return np.asarray(x, np.float32).astype(BF16)


def f64(x):
    return np.asarray(x).astype(np.float64)


B, T, H, KV, D = 4, 1024, 2, 1, 256
G = H // KV
NEG = -1e9


def setup_inputs():
    s = mx_kscale(T)
    keep = np.random.random((1, 1, T, T)) < 0.5
    mask_w = np.where(keep, 1.0 + 0.3 * np.random.standard_normal((1, 1, T, T)), 0.0)
    mask_b = np.where(keep, 0.5 * np.random.standard_normal((1, 1, T, T)) + np.log(s)[None, None, None, :], NEG)
    return {"q_rot": bf(np.random.standard_normal((B, T, H, D))),
            "k_rot": bf(np.random.standard_normal((B, T, KV, D))),
            "v": bf(np.random.standard_normal((B, T, KV, D)) * 2.0 * (s.max() / s)[None, :, None, None]),
            "mask_w": bf(mask_w), "mask_b": bf(mask_b)}


def reference(q_rot, k_rot, v, mask_w, mask_b):
    qg = f64(q_rot).transpose(0, 2, 1, 3).reshape(B, KV, G * T, D)
    kt = f64(k_rot).transpose(0, 2, 3, 1)
    s = (qg @ kt).reshape(B, H, T, T) * (1.0 / np.sqrt(D))
    s = s * f64(mask_w) + f64(mask_b)
    e = np.exp(s - s.max(-1, keepdims=True))
    eq = mxq(e.reshape(B, KV, G * T, T), 3, "e4m3")
    vq = mxq(f64(v).transpose(0, 2, 1, 3), 2, "e4m3")
    o = (eq @ vq).reshape(B, H, T, D) / e.sum(-1, keepdims=True)
    return o.transpose(0, 2, 1, 3)

@@ -1,0 +1,284 @@
+from contextlib import ExitStack
+
+import concourse.masks as masks
+import concourse.mybir as mybir
+
+F32 = mybir.dt.float32
+BF16 = mybir.dt.bfloat16
+U32 = mybir.dt.uint32
+U8 = mybir.dt.uint8
+FP8X4 = mybir.dt.float8_e4m3fn_x4
+ALU = mybir.AluOpType
+ACT = mybir.ActivationFunctionType
+AXIS = mybir.AxisListType
+
+B, T, H, D = 4, 1024, 2, 256
+P = 128
+BANK = 512
+PACK = 4
+PASSES = T // (P * PACK)
+QT = T // P
+DC = D // P
+HALVES = T // BANK
+PAIRS = B * QT
+SCORE_SCALE = 1.0 / 16.0
+KEY_QUARTERS = 4
+QUERY_LEAD = 4
+SCORE_LEAD = 3
+FIRST_SCORE_STEP = -SCORE_LEAD
+
+FLOPS = 2 * 2 * B * H * T * T * D
+
+
+def tile_mistralselfattention_pb_t_kernel(tc, q_rot, k_rot, v, mask_w, mask_b, out):
+    nc = tc.nc
+    with ExitStack() as ctx:
+        ctx.enter_context(tc.manual_schedule())
+        const = ctx.enter_context(tc.tile_pool(name="const", bufs=1))
+        mask_pool = ctx.enter_context(tc.tile_pool(name="masks", bufs=1))
+        raw = ctx.enter_context(tc.tile_pool(name="raw", bufs=B))
+        flipped_pool = ctx.enter_context(tc.tile_pool(name="flipped", bufs=2))
+        value_pool = ctx.enter_context(tc.tile_pool(name="values", bufs=2))
+        masked_pool = ctx.enter_context(tc.tile_pool(name="masked", bufs=3))
+        work = ctx.enter_context(tc.tile_pool(name="work", bufs=2))
+        small = ctx.enter_context(tc.tile_pool(name="small", bufs=4))
+        result_pool = ctx.enter_context(tc.tile_pool(name="result", bufs=3))
+        score_banks = ctx.enter_context(tc.psum_pool(name="score_banks", bufs=H * HALVES))
+        prob_banks = ctx.enter_context(tc.psum_pool(name="prob_banks", bufs=H))
+        out_banks = ctx.enter_context(tc.psum_pool(name="out_banks", bufs=1))
+        operand_banks = ctx.enter_context(tc.psum_pool(name="operand_banks", bufs=1))
+
+        ident_bf16 = const.tile([P, P], BF16)
+        masks.make_identity(nc, ident_bf16[:])
+        ident_f32 = const.tile([P, P], F32)
+        masks.make_identity(nc, ident_f32[:])
+
+        zero = const.tile([P, 1], F32)
+        nc.vector.memset(zero[:], 0.0)
+        one = const.tile([P, 1], F32)
+        nc.scalar.activation(out=one[:], in_=zero[:], func=ACT.Exp)
+
+        q_raw, k_raw, v_raw, weight_rows, bias_rows = {}, {}, {}, {}, {}
+
+        def load_keys(b):
+            k_raw[b] = raw.tile([P, QT, D], BF16, name="k_raw")
+            nc.sync.dma_start(out=k_raw[b][:], in_=k_rot[b].rearrange("(t p) o d -> p t (o d)", p=P))
+
+        def load_queries(b):
+            q_raw[b] = raw.tile([P, QT, H * D], BF16, name="q_raw")
+            nc.sync.dma_start(out=q_raw[b][:], in_=q_rot[b].rearrange("(t p) h d -> p t (h d)", p=P))
+
+        def load_values(b):
+            v_raw[b] = raw.tile([P, PASSES, PACK, D], BF16, name="v_raw")
+            nc.sync.dma_start(
+                out=v_raw[b][:].rearrange("p g t d -> p g (t d)"),
+                in_=v[b].rearrange("(g p t) o d -> p g (t o d)", p=P, t=PACK),
+            )
+
+        def load_masks(qt):
+            rows = slice(qt * P, (qt + 1) * P)
+            weight_rows[qt] = mask_pool.tile([P, T], BF16, name="weight_rows%d" % qt)
+            nc.sync.dma_start(out=weight_rows[qt][:], in_=mask_w[0, 0, rows, :])
+            bias_rows[qt] = mask_pool.tile([P, T], BF16, name="bias_rows%d" % qt)
+            nc.sync.dma_start(out=bias_rows[qt][:], in_=mask_b[0, 0, rows, :])
+
+        load_keys(0)
+        load_queries(0)
+        load_masks(0)
+        load_values(0)
+        load_keys(1)
+        for qt in range(1, QT):
+            load_masks(qt)
+        load_queries(1)
+        load_values(1)
+        for b in range(2, B):
+            load_keys(b)
+            load_queries(b)
+            load_values(b)
+
+        q_flipped, k_flipped, v_grouped, v_codes, v_scales = {}, {}, {}, {}, {}
+        scores, masked, neg_max, row_sum, inv_sum = {}, {}, {}, {}, {}
+        probs, probs_flipped, probs_grouped, prob_codes, prob_scales, products = {}, {}, {}, {}, {}, {}
+
+        def live(pair):
+            return 0 <= pair < PAIRS
+
+        def flip_operands(step):
+            pair = step + QUERY_LEAD
+            next_b, quarter = step // QT + 1, step % QT
+            with_keys = quarter < KEY_QUARTERS and 0 <= next_b < B
+            if not (live(pair) or with_keys):
+                return
+            if step < FIRST_SCORE_STEP:
+                bank = score_banks.tile([P, 2, DC, 2, P], BF16, name="early_operand_bank", tag="score_bank")
+            else:
+                bank = operand_banks.tile([P, 2, DC, 2, P], BF16, name="operand_bank")
+            if live(pair):
+                b, qt = divmod(pair, QT)
+                if qt == 0:
+                    q_flipped[b] = flipped_pool.tile([P, DC, H, T], BF16, name="q_flipped")
+                for c in range(DC):
+                    for h in range(H):
+                        first = h * D + c * P
+                        nc.tensor.transpose(bank[:, 0, c, h, :], q_raw[b][:, qt, first : first + P], ident_bf16[:])
+                nc.scalar.copy(out=q_flipped[b][:, :, :, qt * P : (qt + 1) * P], in_=bank[:, 0])
+            if with_keys:
+                if quarter == 0:
+                    k_flipped[next_b] = flipped_pool.tile([P, DC, T], BF16, name="k_flipped")
+                for c in range(DC):
+                    for j in range(2):
+                        nc.tensor.transpose(
+                            bank[:, 1, c, j, :], k_raw[next_b][:, 2 * quarter + j, c * P : (c + 1) * P], ident_bf16[:]
+                        )
+                nc.scalar.copy(
+                    out=k_flipped[next_b][:, :, 2 * quarter * P : 2 * (quarter + 1) * P],
+                    in_=bank[:, 1].rearrange("p c j k -> p c (j k)"),
+                )
+
+        def group_values(b):
+            v_grouped[b] = value_pool.tile([P, PASSES, D, PACK], BF16, name="v_grouped", align_bytes=64)
+            nc.scalar.copy(out=v_grouped[b][:], in_=v_raw[b][:].rearrange("p g t d -> p g d t"))
+
+        def quantise_values(b):
+            v_codes[b] = value_pool.tile([P, PASSES, D], U32, name="v_codes", align_bytes=64)
+            v_scales[b] = value_pool.tile([P, PASSES, D], U8, name="v_scales", align_bytes=64)
+            nc.vector.quantize_mx(
+                out=v_codes[b][:].rearrange("p g d -> p (g d)").bitcast(FP8X4),
+                scales=v_scales[b][:].rearrange("p g d -> p (g d)"),
+                in_=v_grouped[b][:].rearrange("p g d t -> p (g d t)"),
+            )
+
+        def score_matmuls(pair):
+            b, qt = divmod(pair, QT)
+            for h in range(H):
+                for half in range(HALVES):
+                    bank = score_banks.tile([P, BANK], F32, name="score_bank")
+                    scores[(pair, h, half)] = bank
+                    for c in range(DC):
+                        nc.tensor.matmul(
+                            out=bank[:],
+                            lhsT=q_flipped[b][:, c, h, qt * P : (qt + 1) * P],
+                            rhs=k_flipped[b][:, c, half * BANK : (half + 1) * BANK],
+                            start=(c == 0),
+                            stop=(c == DC - 1),
+                        )
+
+        def weigh(pair):
+            qt = pair % QT
+            masked[pair] = masked_pool.tile([P, H, T], F32, name="masked")
+            for h in range(H):
+                for half in range(HALVES):
+                    keys = slice(half * BANK, (half + 1) * BANK)
+                    nc.vector.scalar_tensor_tensor(
+                        out=masked[pair][:, h, keys],
+                        in0=scores[(pair, h, half)][:],
+                        scalar=SCORE_SCALE,
+                        in1=weight_rows[qt][:, keys],
+                        op0=ALU.mult,
+                        op1=ALU.mult,
+                    )
+
+        def add_bias(pair):
+            qt = pair % QT
+            nc.gpsimd.tensor_tensor(
+                out=masked[pair][:],
+                in0=masked[pair][:],
+                in1=bias_rows[qt][:].unsqueeze(1).to_broadcast([P, H, T]),
+                op=ALU.add,
+            )
+
+        def row_maxima(pair):
+            neg_max[pair] = small.tile([P, H], F32, name="neg_max")
+            nc.vector.tensor_reduce(out=neg_max[pair][:], in_=masked[pair][:], axis=AXIS.X, op=ALU.max, negate=True)
+
+        def exponentials(pair):
+            probs[pair] = work.tile([P, H, T], BF16, name="probs")
+            row_sum[pair] = small.tile([P, H], F32, name="row_sum")
+            for h in range(H):
+                nc.scalar.activation(
+                    out=probs[pair][:, h, :],
+                    in_=masked[pair][:, h, :],
+                    func=ACT.Exp,
+                    bias=neg_max[pair][:, h : h + 1],
+                    scale=1.0,
+                    accum_out=row_sum[pair][:, h : h + 1],
+                )
+
+        def flip_probs(pair):
+            for h in range(H):
+                bank = prob_banks.tile([P, PASSES * 2, P], F32, name="prob_bank")
+                probs_flipped[(pair, h)] = bank
+                words = probs[pair][:, h, :].bitcast(F32)
+                for g in range(PASSES):
+                    for u in range(2):
+                        first = g * 2 * P + u
+                        nc.tensor.transpose(bank[:, 2 * g + u, :], words[:, first : (g + 1) * 2 * P : 2], ident_f32[:])
+
+        def group_probs(pair):
+            probs_grouped[pair] = work.tile([P, H, PASSES, P, PACK], BF16, name="probs_grouped", align_bytes=64)
+            for h in range(H):
+                nc.scalar.copy(
+                    out=probs_grouped[pair][:, h].bitcast(F32),
+                    in_=probs_flipped[(pair, h)][:].rearrange("p (g u) q -> p g q u", u=2),
+                )
+
+        def quantise_probs(pair):
+            prob_codes[pair] = work.tile([P, H, PASSES, P], U32, name="prob_codes", align_bytes=64)
+            prob_scales[pair] = work.tile([P, H, PASSES, P], U8, name="prob_scales", align_bytes=64)
+            nc.vector.quantize_mx(
+                out=prob_codes[pair][:].rearrange("p h g q -> p (h g q)").bitcast(FP8X4),
+                scales=prob_scales[pair][:].rearrange("p h g q -> p (h g q)"),
+                in_=probs_grouped[pair][:].rearrange("p h g q t -> p (h g q t)"),
+            )
+            inv_sum[pair] = small.tile([P, H], F32, name="inv_sum")
+            nc.vector.reciprocal(out=inv_sum[pair][:], in_=row_sum[pair][:])
+
+        def weighted_values(pair):
+            b = pair // QT
+            products[pair] = out_banks.tile([P, H, D], F32, name="out_bank")
+            for h in range(H):
+                for g in range(PASSES):
+                    nc.tensor.matmul_mx(
+                        out=products[pair][:, h, :],
+                        lhsT=prob_codes[pair][:, h, g, :].bitcast(FP8X4),
+                        lhsT_scale=prob_scales[pair][:, h, g, :],
+                        rhs=v_codes[b][:, g, :].bitcast(FP8X4),
+                        rhs_scale=v_scales[b][:, g, :],
+                        start=(g == 0),
+                        stop=(g == PASSES - 1),
+                    )
+
+        def normalise_and_store(pair):
+            b, qt = divmod(pair, QT)
+            result = result_pool.tile([P, H, D], F32, name="result")
+            for h in range(H):
+                nc.scalar.activation(
+                    out=result[:, h, :], in_=products[pair][:, h, :], func=ACT.Copy, scale=inv_sum[pair][:, h : h + 1]
+                )
+            nc.sync.dma_start(out=out[b, qt * P : (qt + 1) * P, :, :], in_=result[:])
+
+        for step in range(-QT, PAIRS + 3):
+            if live(step):
+                row_maxima(step)
+                exponentials(step)
+            if live(step - 1):
+                group_probs(step - 1)
+            if live(step - 3):
+                normalise_and_store(step - 3)
+            flip_operands(step)
+            if (step + 1) % QT == 0 and live(step + 1):
+                group_values((step + 1) // QT)
+            if live(step + 2):
+                weigh(step + 2)
+            if live(step + SCORE_LEAD):
+                score_matmuls(step + SCORE_LEAD)
+            if live(step + 1):
+                add_bias(step + 1)
+            if live(step - 2):
+                quantise_probs(step - 2)
+            if step % QT == 0 and live(step):
+                quantise_values(step // QT)
+            if live(step):
+                flip_probs(step)
+            if live(step - 2):
+                weighted_values(step - 2)

@@ -23,6 +23,7 @@ HALVES = T // BANK
 PAIRS = B * QT
 SCORE_SCALE = 1.0 / 16.0
 KEY_QUARTERS = 4
+VALUE_PIECES = 4
 QUERY_LEAD = 4
 SCORE_LEAD = 3
 FIRST_SCORE_STEP = -SCORE_LEAD
@@ -135,9 +136,14 @@ def tile_mistralselfattention_pb_t_kernel(tc, q_rot, k_rot, v, mask_w, mask_b, o
                     in_=bank[:, 1].rearrange("p c j k -> p c (j k)"),
                 )
 
-        def group_values(b):
-            v_grouped[b] = value_pool.tile([P, PASSES, D, PACK], BF16, name="v_grouped", align_bytes=64)
-            nc.scalar.copy(out=v_grouped[b][:], in_=v_raw[b][:].rearrange("p g t d -> p g d t"))
+        def group_values(b, piece):
+            if piece == 0:
+                v_grouped[b] = value_pool.tile([P, PASSES, D, PACK], BF16, name="v_grouped", align_bytes=64)
+            width = D // VALUE_PIECES
+            columns = slice(piece * width, (piece + 1) * width)
+            nc.scalar.copy(
+                out=v_grouped[b][:, :, columns, :], in_=v_raw[b][:, :, :, columns].rearrange("p g t d -> p g d t")
+            )
 
         def quantise_values(b):
             v_codes[b] = value_pool.tile([P, PASSES, D], U32, name="v_codes", align_bytes=64)
@@ -265,13 +271,16 @@ def tile_mistralselfattention_pb_t_kernel(tc, q_rot, k_rot, v, mask_w, mask_b, o
                 group_probs(step - 1)
             if live(step - 3):
                 normalise_and_store(step - 3)
-            flip_operands(step)
-            if (step + 1) % QT == 0 and live(step + 1):
-                group_values((step + 1) // QT)
             if live(step + 2):
                 weigh(step + 2)
             if live(step + SCORE_LEAD):
                 score_matmuls(step + SCORE_LEAD)
+            flip_operands(step)
+            if step == -1:
+                for piece in range(VALUE_PIECES):
+                    group_values(0, piece)
+            elif step >= 0 and step % QT >= KEY_QUARTERS and step // QT + 1 < B:
+                group_values(step // QT + 1, step % QT - KEY_QUARTERS)
             if live(step + 1):
                 add_bias(step + 1)
             if live(step - 2):

@@ -99,7 +99,7 @@ def tile_mistralselfattention_pb_t_kernel(tc, q_rot, k_rot, v, mask_w, mask_b, o
 
         q_flipped, k_flipped, v_grouped, v_codes, v_scales = {}, {}, {}, {}, {}
         scores, masked, neg_max, row_sum, inv_sum = {}, {}, {}, {}, {}
-        probs, probs_flipped, probs_grouped, prob_codes, prob_scales, products = {}, {}, {}, {}, {}, {}
+        probs, probs_flipped, probs_grouped, prob_codes, prob_scales, products, result = {}, {}, {}, {}, {}, {}, {}
 
         def live(pair):
             return 0 <= pair < PAIRS
@@ -193,9 +193,17 @@ def tile_mistralselfattention_pb_t_kernel(tc, q_rot, k_rot, v, mask_w, mask_b, o
                 op=ALU.add,
             )
 
-        def row_maxima(pair):
-            neg_max[pair] = small.tile([P, H], F32, name="neg_max")
-            nc.vector.tensor_reduce(out=neg_max[pair][:], in_=masked[pair][:], axis=AXIS.X, op=ALU.max, negate=True)
+        def add_bias_to_head(pair, h, engine):
+            scores_of_head = masked[pair][:, h, :]
+            engine.tensor_tensor(out=scores_of_head, in0=scores_of_head, in1=bias_rows[pair % QT][:], op=ALU.add)
+
+        def row_maxima(pair, first=0, heads=H):
+            if first == 0:
+                neg_max[pair] = small.tile([P, H], F32, name="neg_max")
+            of_heads = slice(first, first + heads)
+            nc.vector.tensor_reduce(
+                out=neg_max[pair][:, of_heads], in_=masked[pair][:, of_heads, :], axis=AXIS.X, op=ALU.max, negate=True
+            )
 
         def exponentials(pair):
             probs[pair] = work.tile([P, H, T], BF16, name="probs")
@@ -210,9 +218,12 @@ def tile_mistralselfattention_pb_t_kernel(tc, q_rot, k_rot, v, mask_w, mask_b, o
                     accum_out=row_sum[pair][:, h : h + 1],
                 )
 
-        def flip_probs(pair):
+        def flip_probs(pair, spare_banks=False):
             for h in range(H):
-                bank = prob_banks.tile([P, PASSES * 2, P], F32, name="prob_bank")
+                if spare_banks:
+                    bank = score_banks.tile([P, PASSES * 2, P], F32, name="spare_prob_bank", tag="score_bank")
+                else:
+                    bank = prob_banks.tile([P, PASSES * 2, P], F32, name="prob_bank")
                 probs_flipped[(pair, h)] = bank
                 words = probs[pair][:, h, :].bitcast(F32)
                 for g in range(PASSES):
@@ -220,29 +231,37 @@ def tile_mistralselfattention_pb_t_kernel(tc, q_rot, k_rot, v, mask_w, mask_b, o
                         first = g * 2 * P + u
                         nc.tensor.transpose(bank[:, 2 * g + u, :], words[:, first : (g + 1) * 2 * P : 2], ident_f32[:])
 
-        def group_probs(pair):
+        def group_probs(pair, copy=nc.scalar.copy):
             probs_grouped[pair] = work.tile([P, H, PASSES, P, PACK], BF16, name="probs_grouped", align_bytes=64)
             for h in range(H):
-                nc.scalar.copy(
+                copy(
                     out=probs_grouped[pair][:, h].bitcast(F32),
                     in_=probs_flipped[(pair, h)][:].rearrange("p (g u) q -> p g q u", u=2),
                 )
 
-        def quantise_probs(pair):
-            prob_codes[pair] = work.tile([P, H, PASSES, P], U32, name="prob_codes", align_bytes=64)
-            prob_scales[pair] = work.tile([P, H, PASSES, P], U8, name="prob_scales", align_bytes=64)
+        def quantise_probs(pair, first=0, heads=H):
+            if first == 0:
+                prob_codes[pair] = work.tile([P, H, PASSES, P], U32, name="prob_codes", align_bytes=64)
+                prob_scales[pair] = work.tile([P, H, PASSES, P], U8, name="prob_scales", align_bytes=64)
+            of_heads = slice(first, first + heads)
             nc.vector.quantize_mx(
-                out=prob_codes[pair][:].rearrange("p h g q -> p (h g q)").bitcast(FP8X4),
-                scales=prob_scales[pair][:].rearrange("p h g q -> p (h g q)"),
-                in_=probs_grouped[pair][:].rearrange("p h g q t -> p (h g q t)"),
+                out=prob_codes[pair][:, of_heads].rearrange("p h g q -> p (h g q)").bitcast(FP8X4),
+                scales=prob_scales[pair][:, of_heads].rearrange("p h g q -> p (h g q)"),
+                in_=probs_grouped[pair][:, of_heads].rearrange("p h g q t -> p (h g q t)"),
             )
-            inv_sum[pair] = small.tile([P, H], F32, name="inv_sum")
-            nc.vector.reciprocal(out=inv_sum[pair][:], in_=row_sum[pair][:])
+            if first == 0:
+                inv_sum[pair] = small.tile([P, H], F32, name="inv_sum")
+                nc.vector.reciprocal(out=inv_sum[pair][:], in_=row_sum[pair][:])
 
-        def weighted_values(pair):
+        def product_bank(pair, spare_bank=False):
+            if spare_bank:
+                products[pair] = score_banks.tile([P, H, D], F32, name="spare_out_bank", tag="score_bank")
+            else:
+                products[pair] = out_banks.tile([P, H, D], F32, name="out_bank")
+
+        def weighted_values(pair, heads=range(H)):
             b = pair // QT
-            products[pair] = out_banks.tile([P, H, D], F32, name="out_bank")
-            for h in range(H):
+            for h in heads:
                 for g in range(PASSES):
                     nc.tensor.matmul_mx(
                         out=products[pair][:, h, :],
@@ -254,16 +273,28 @@ def tile_mistralselfattention_pb_t_kernel(tc, q_rot, k_rot, v, mask_w, mask_b, o
                         stop=(g == PASSES - 1),
                     )
 
-        def normalise_and_store(pair):
-            b, qt = divmod(pair, QT)
-            result = result_pool.tile([P, H, D], F32, name="result")
-            for h in range(H):
+        def normalise(pair, h, on_vector=False):
+            if h == 0:
+                result[pair] = result_pool.tile([P, H, D], F32, name="result")
+            factor = inv_sum[pair][:, h : h + 1]
+            if on_vector:
+                nc.vector.tensor_scalar_mul(out=result[pair][:, h, :], in0=products[pair][:, h, :], scalar1=factor)
+            else:
                 nc.scalar.activation(
-                    out=result[:, h, :], in_=products[pair][:, h, :], func=ACT.Copy, scale=inv_sum[pair][:, h : h + 1]
+                    out=result[pair][:, h, :], in_=products[pair][:, h, :], func=ACT.Copy, scale=factor
                 )
-            nc.sync.dma_start(out=out[b, qt * P : (qt + 1) * P, :, :], in_=result[:])
 
-        for step in range(-QT, PAIRS + 3):
+        def store(pair):
+            b, qt = divmod(pair, QT)
+            nc.sync.dma_start(out=out[b, qt * P : (qt + 1) * P, :, :], in_=result[pair][:])
+
+        def normalise_and_store(pair, on_vector=False):
+            for h in range(H):
+                normalise(pair, h, on_vector)
+            store(pair)
+
+        last = PAIRS - 1
+        for step in range(-QT, last - 1):
             if live(step):
                 row_maxima(step)
                 exponentials(step)
@@ -290,4 +321,38 @@ def tile_mistralselfattention_pb_t_kernel(tc, q_rot, k_rot, v, mask_w, mask_b, o
             if live(step):
                 flip_probs(step)
             if live(step - 2):
+                product_bank(step - 2)
                 weighted_values(step - 2)
+
+        row_maxima(last - 1)
+        group_probs(last - 2)
+        add_bias_to_head(last, 0, nc.gpsimd)
+        add_bias_to_head(last, 1, nc.vector)
+        exponentials(last - 1)
+        flip_probs(last - 1)
+        for h in range(H):
+            row_maxima(last, h, 1)
+        exponentials(last)
+        flip_probs(last, spare_banks=True)
+        normalise_and_store(last - 4, on_vector=True)
+        quantise_probs(last - 3)
+        quantise_probs(last - 2)
+        product_bank(last - 3)
+        weighted_values(last - 3)
+        product_bank(last - 2, spare_bank=True)
+        weighted_values(last - 2)
+        group_probs(last - 1, copy=nc.vector.tensor_copy)
+        group_probs(last)
+        normalise_and_store(last - 3)
+        normalise_and_store(last - 2)
+        quantise_probs(last - 1)
+        product_bank(last - 1, spare_bank=True)
+        weighted_values(last - 1)
+        product_bank(last)
+        for h in range(H):
+            quantise_probs(last, h, 1)
+            weighted_values(last, [h])
+        normalise_and_store(last - 1)
+        normalise(last, 0)
+        normalise(last, 1, on_vector=True)
+        store(last)

@@ -19,6 +19,7 @@ PACK = 4
 PASSES = T // (P * PACK)
 QT = T // P
 DC = D // P
+WORDS = H * T // PACK
 HALVES = T // BANK
 PAIRS = B * QT
 SCORE_SCALE = 1.0 / 16.0
@@ -43,7 +44,7 @@ def tile_mistralselfattention_pb_t_kernel(tc, q_rot, k_rot, v, mask_w, mask_b, o
         masked_pool = ctx.enter_context(tc.tile_pool(name="masked", bufs=3))
         work = ctx.enter_context(tc.tile_pool(name="work", bufs=2))
         small = ctx.enter_context(tc.tile_pool(name="small", bufs=4))
-        result_pool = ctx.enter_context(tc.tile_pool(name="result", bufs=3))
+        result_pool = ctx.enter_context(tc.tile_pool(name="result", bufs=6))
         score_banks = ctx.enter_context(tc.psum_pool(name="score_banks", bufs=H * HALVES))
         prob_banks = ctx.enter_context(tc.psum_pool(name="prob_banks", bufs=H))
         out_banks = ctx.enter_context(tc.psum_pool(name="out_banks", bufs=1))
@@ -97,7 +98,7 @@ def tile_mistralselfattention_pb_t_kernel(tc, q_rot, k_rot, v, mask_w, mask_b, o
             load_queries(b)
             load_values(b)
 
-        q_flipped, k_flipped, v_grouped, v_codes, v_scales = {}, {}, {}, {}, {}
+        q_flipped, k_flipped, v_with_probs, v_grouped, v_codes, v_scales = {}, {}, {}, {}, {}, {}
         scores, masked, neg_max, row_sum, inv_sum = {}, {}, {}, {}, {}
         probs, probs_flipped, probs_grouped, prob_codes, prob_scales, products, result = {}, {}, {}, {}, {}, {}, {}
 
@@ -138,20 +139,12 @@ def tile_mistralselfattention_pb_t_kernel(tc, q_rot, k_rot, v, mask_w, mask_b, o
 
         def group_values(b, piece):
             if piece == 0:
-                v_grouped[b] = value_pool.tile([P, PASSES, D, PACK], BF16, name="v_grouped", align_bytes=64)
+                v_with_probs[b] = value_pool.tile([P, 2, T * H], BF16, name="v_with_probs", align_bytes=64)
+                v_grouped[b] = v_with_probs[b][:, 1].rearrange("p (g d t) -> p g d t", g=PASSES, t=PACK)
             width = D // VALUE_PIECES
             columns = slice(piece * width, (piece + 1) * width)
             nc.scalar.copy(
                 out=v_grouped[b][:, :, columns, :], in_=v_raw[b][:, :, :, columns].rearrange("p g t d -> p g d t")
-            )
-
-        def quantise_values(b):
-            v_codes[b] = value_pool.tile([P, PASSES, D], U32, name="v_codes", align_bytes=64)
-            v_scales[b] = value_pool.tile([P, PASSES, D], U8, name="v_scales", align_bytes=64)
-            nc.vector.quantize_mx(
-                out=v_codes[b][:].rearrange("p g d -> p (g d)").bitcast(FP8X4),
-                scales=v_scales[b][:].rearrange("p g d -> p (g d)"),
-                in_=v_grouped[b][:].rearrange("p g d t -> p (g d t)"),
             )
 
         def score_matmuls(pair):
@@ -232,26 +225,45 @@ def tile_mistralselfattention_pb_t_kernel(tc, q_rot, k_rot, v, mask_w, mask_b, o
                         nc.tensor.transpose(bank[:, 2 * g + u, :], words[:, first : (g + 1) * 2 * P : 2], ident_f32[:])
 
         def group_probs(pair, copy=nc.scalar.copy):
-            probs_grouped[pair] = work.tile([P, H, PASSES, P, PACK], BF16, name="probs_grouped", align_bytes=64)
+            if pair % QT == 0:
+                probs_grouped[pair] = v_with_probs[pair // QT][:, 0].rearrange("p (h n) -> p h n", h=H)
+            else:
+                probs_grouped[pair] = work.tile([P, H, T], BF16, name="probs_grouped", align_bytes=64)[:]
             for h in range(H):
                 copy(
-                    out=probs_grouped[pair][:, h].bitcast(F32),
+                    out=probs_grouped[pair][:, h].bitcast(F32).rearrange("p (g q u) -> p g q u", g=PASSES, u=2),
                     in_=probs_flipped[(pair, h)][:].rearrange("p (g u) q -> p g q u", u=2),
                 )
 
+        def invert_sums(pair):
+            inv_sum[pair] = small.tile([P, H], F32, name="inv_sum")
+            nc.vector.reciprocal(out=inv_sum[pair][:], in_=row_sum[pair][:])
+
+        def quantise(codes, scales, values):
+            nc.vector.quantize_mx(out=codes.bitcast(FP8X4), scales=scales, in_=values)
+
+        def quantise_probs_and_values(pair):
+            b = pair // QT
+            codes = value_pool.tile([P, 2, WORDS], U32, name="codes_with_v", align_bytes=64)
+            scales = value_pool.tile([P, 2, WORDS], U8, name="scales_with_v", align_bytes=64)
+            quantise(
+                codes[:].rearrange("p i w -> p (i w)"),
+                scales[:].rearrange("p i w -> p (i w)"),
+                v_with_probs[b][:].rearrange("p i n -> p (i n)"),
+            )
+            prob_codes[pair], prob_scales[pair] = codes[:, 0], scales[:, 0]
+            v_codes[b], v_scales[b] = codes[:, 1], scales[:, 1]
+
         def quantise_probs(pair, first=0, heads=H):
             if first == 0:
-                prob_codes[pair] = work.tile([P, H, PASSES, P], U32, name="prob_codes", align_bytes=64)
-                prob_scales[pair] = work.tile([P, H, PASSES, P], U8, name="prob_scales", align_bytes=64)
-            of_heads = slice(first, first + heads)
-            nc.vector.quantize_mx(
-                out=prob_codes[pair][:, of_heads].rearrange("p h g q -> p (h g q)").bitcast(FP8X4),
-                scales=prob_scales[pair][:, of_heads].rearrange("p h g q -> p (h g q)"),
-                in_=probs_grouped[pair][:, of_heads].rearrange("p h g q t -> p (h g q t)"),
+                prob_codes[pair] = work.tile([P, WORDS], U32, name="prob_codes", align_bytes=64)[:]
+                prob_scales[pair] = work.tile([P, WORDS], U8, name="prob_scales", align_bytes=64)[:]
+            words = slice(first * WORDS // H, (first + heads) * WORDS // H)
+            quantise(
+                prob_codes[pair][:, words],
+                prob_scales[pair][:, words],
+                probs_grouped[pair][:, first : first + heads].rearrange("p h n -> p (h n)"),
             )
-            if first == 0:
-                inv_sum[pair] = small.tile([P, H], F32, name="inv_sum")
-                nc.vector.reciprocal(out=inv_sum[pair][:], in_=row_sum[pair][:])
 
         def product_bank(pair, spare_bank=False):
             if spare_bank:
@@ -263,12 +275,15 @@ def tile_mistralselfattention_pb_t_kernel(tc, q_rot, k_rot, v, mask_w, mask_b, o
             b = pair // QT
             for h in heads:
                 for g in range(PASSES):
+                    first = (h * PASSES + g) * P
+                    queries = slice(first, first + P)
+                    columns = slice(g * D, (g + 1) * D)
                     nc.tensor.matmul_mx(
                         out=products[pair][:, h, :],
-                        lhsT=prob_codes[pair][:, h, g, :].bitcast(FP8X4),
-                        lhsT_scale=prob_scales[pair][:, h, g, :],
-                        rhs=v_codes[b][:, g, :].bitcast(FP8X4),
-                        rhs_scale=v_scales[b][:, g, :],
+                        lhsT=prob_codes[pair][:, queries].bitcast(FP8X4),
+                        lhsT_scale=prob_scales[pair][:, queries],
+                        rhs=v_codes[b][:, columns].bitcast(FP8X4),
+                        rhs_scale=v_scales[b][:, columns],
                         start=(g == 0),
                         stop=(g == PASSES - 1),
                     )
@@ -315,9 +330,11 @@ def tile_mistralselfattention_pb_t_kernel(tc, q_rot, k_rot, v, mask_w, mask_b, o
             if live(step + 1):
                 add_bias(step + 1)
             if live(step - 2):
-                quantise_probs(step - 2)
-            if step % QT == 0 and live(step):
-                quantise_values(step // QT)
+                invert_sums(step - 2)
+                if (step - 2) % QT == 0:
+                    quantise_probs_and_values(step - 2)
+                else:
+                    quantise_probs(step - 2)
             if live(step):
                 flip_probs(step)
             if live(step - 2):
@@ -335,6 +352,8 @@ def tile_mistralselfattention_pb_t_kernel(tc, q_rot, k_rot, v, mask_w, mask_b, o
         exponentials(last)
         flip_probs(last, spare_banks=True)
         normalise_and_store(last - 4, on_vector=True)
+        for pair in range(last - 3, last + 1):
+            invert_sums(pair)
         quantise_probs(last - 3)
         quantise_probs(last - 2)
         product_bank(last - 3)

@@ -27,7 +27,6 @@ KEY_QUARTERS = 4
 VALUE_PIECES = 4
 QUERY_LEAD = 4
 SCORE_LEAD = 3
-FIRST_SCORE_STEP = -SCORE_LEAD
 
 FLOPS = 2 * 2 * B * H * T * T * D
 
@@ -62,13 +61,21 @@ def tile_mistralselfattention_pb_t_kernel(tc, q_rot, k_rot, v, mask_w, mask_b, o
 
         q_raw, k_raw, v_raw, weight_rows, bias_rows = {}, {}, {}, {}, {}
 
-        def load_keys(b):
-            k_raw[b] = raw.tile([P, QT, D], BF16, name="k_raw")
-            nc.sync.dma_start(out=k_raw[b][:], in_=k_rot[b].rearrange("(t p) o d -> p t (o d)", p=P))
+        def load_keys(b, first=0, tiles=QT):
+            if first == 0:
+                k_raw[b] = raw.tile([P, QT, D], BF16, name="k_raw")
+            nc.sync.dma_start(
+                out=k_raw[b][:, first : first + tiles, :],
+                in_=k_rot[b, first * P : (first + tiles) * P].rearrange("(t p) o d -> p t (o d)", p=P),
+            )
 
-        def load_queries(b):
-            q_raw[b] = raw.tile([P, QT, H * D], BF16, name="q_raw")
-            nc.sync.dma_start(out=q_raw[b][:], in_=q_rot[b].rearrange("(t p) h d -> p t (h d)", p=P))
+        def load_queries(b, first=0, tiles=QT):
+            if first == 0:
+                q_raw[b] = raw.tile([P, QT, H * D], BF16, name="q_raw")
+            nc.sync.dma_start(
+                out=q_raw[b][:, first : first + tiles, :],
+                in_=q_rot[b, first * P : (first + tiles) * P].rearrange("(t p) h d -> p t (h d)", p=P),
+            )
 
         def load_values(b):
             v_raw[b] = raw.tile([P, PASSES, PACK, D], BF16, name="v_raw")
@@ -84,12 +91,16 @@ def tile_mistralselfattention_pb_t_kernel(tc, q_rot, k_rot, v, mask_w, mask_b, o
             bias_rows[qt] = mask_pool.tile([P, T], BF16, name="bias_rows%d" % qt)
             nc.sync.dma_start(out=bias_rows[qt][:], in_=mask_b[0, 0, rows, :])
 
-        load_keys(0)
-        load_queries(0)
+        load_keys(0, 0, QT // 2)
+        load_queries(0, 0, 1)
+        load_keys(0, QT // 2, QT // 2)
         load_masks(0)
+        load_queries(0, 1, QT - 1)
+        load_masks(1)
         load_values(0)
+        load_masks(2)
         load_keys(1)
-        for qt in range(1, QT):
+        for qt in range(3, QT):
             load_masks(qt)
         load_queries(1)
         load_values(1)
@@ -105,37 +116,44 @@ def tile_mistralselfattention_pb_t_kernel(tc, q_rot, k_rot, v, mask_w, mask_b, o
         def live(pair):
             return 0 <= pair < PAIRS
 
+        def operand_bank(idle_score_bank=False):
+            if idle_score_bank:
+                return score_banks.tile([P, 2, DC, 2, P], BF16, name="early_operand_bank", tag="score_bank")
+            return operand_banks.tile([P, 2, DC, 2, P], BF16, name="operand_bank")
+
+        def flip_queries(pair, bank, copy=nc.scalar.copy):
+            b, qt = divmod(pair, QT)
+            if qt == 0:
+                q_flipped[b] = flipped_pool.tile([P, DC, H, T], BF16, name="q_flipped")
+            for c in range(DC):
+                for h in range(H):
+                    first = h * D + c * P
+                    nc.tensor.transpose(bank[:, 0, c, h, :], q_raw[b][:, qt, first : first + P], ident_bf16[:])
+            copy(out=q_flipped[b][:, :, :, qt * P : (qt + 1) * P], in_=bank[:, 0])
+
+        def flip_keys(b, quarter, bank, copy=nc.scalar.copy):
+            if quarter == 0:
+                k_flipped[b] = flipped_pool.tile([P, DC, T], BF16, name="k_flipped")
+            for c in range(DC):
+                for j in range(2):
+                    nc.tensor.transpose(
+                        bank[:, 1, c, j, :], k_raw[b][:, 2 * quarter + j, c * P : (c + 1) * P], ident_bf16[:]
+                    )
+            copy(
+                out=k_flipped[b][:, :, 2 * quarter * P : 2 * (quarter + 1) * P],
+                in_=bank[:, 1].rearrange("p c j k -> p c (j k)"),
+            )
+
         def flip_operands(step):
             pair = step + QUERY_LEAD
             next_b, quarter = step // QT + 1, step % QT
-            with_keys = quarter < KEY_QUARTERS and 0 <= next_b < B
-            if not (live(pair) or with_keys):
-                return
-            if step < FIRST_SCORE_STEP:
-                bank = score_banks.tile([P, 2, DC, 2, P], BF16, name="early_operand_bank", tag="score_bank")
-            else:
-                bank = operand_banks.tile([P, 2, DC, 2, P], BF16, name="operand_bank")
+            with_keys = quarter < KEY_QUARTERS and next_b < B
+            if live(pair) or with_keys:
+                bank = operand_bank()
             if live(pair):
-                b, qt = divmod(pair, QT)
-                if qt == 0:
-                    q_flipped[b] = flipped_pool.tile([P, DC, H, T], BF16, name="q_flipped")
-                for c in range(DC):
-                    for h in range(H):
-                        first = h * D + c * P
-                        nc.tensor.transpose(bank[:, 0, c, h, :], q_raw[b][:, qt, first : first + P], ident_bf16[:])
-                nc.scalar.copy(out=q_flipped[b][:, :, :, qt * P : (qt + 1) * P], in_=bank[:, 0])
+                flip_queries(pair, bank)
             if with_keys:
-                if quarter == 0:
-                    k_flipped[next_b] = flipped_pool.tile([P, DC, T], BF16, name="k_flipped")
-                for c in range(DC):
-                    for j in range(2):
-                        nc.tensor.transpose(
-                            bank[:, 1, c, j, :], k_raw[next_b][:, 2 * quarter + j, c * P : (c + 1) * P], ident_bf16[:]
-                        )
-                nc.scalar.copy(
-                    out=k_flipped[next_b][:, :, 2 * quarter * P : 2 * (quarter + 1) * P],
-                    in_=bank[:, 1].rearrange("p c j k -> p c (j k)"),
-                )
+                flip_keys(next_b, quarter, bank)
 
         def group_values(b, piece):
             if piece == 0:
@@ -162,10 +180,11 @@ def tile_mistralselfattention_pb_t_kernel(tc, q_rot, k_rot, v, mask_w, mask_b, o
                             stop=(c == DC - 1),
                         )
 
-        def weigh(pair):
+        def weigh(pair, heads=range(H)):
             qt = pair % QT
-            masked[pair] = masked_pool.tile([P, H, T], F32, name="masked")
-            for h in range(H):
+            if 0 in heads:
+                masked[pair] = masked_pool.tile([P, H, T], F32, name="masked")
+            for h in heads:
                 for half in range(HALVES):
                     keys = slice(half * BANK, (half + 1) * BANK)
                     nc.vector.scalar_tensor_tensor(
@@ -308,35 +327,56 @@ def tile_mistralselfattention_pb_t_kernel(tc, q_rot, k_rot, v, mask_w, mask_b, o
                 normalise(pair, h, on_vector)
             store(pair)
 
+        flip_keys(0, 0, operand_bank(idle_score_bank=True))
+        flip_keys(0, 1, operand_bank(idle_score_bank=True), copy=nc.vector.tensor_copy)
+        flip_queries(0, operand_bank(idle_score_bank=True))
+        flip_keys(0, 2, operand_bank(idle_score_bank=True), copy=nc.vector.tensor_copy)
+        flip_keys(0, 3, operand_bank())
+
+        score_matmuls(0)
+        flip_queries(1, operand_bank())
+        weigh(0, [0])
+        add_bias_to_head(0, 0, nc.gpsimd)
+        weigh(0, [1])
+        score_matmuls(1)
+        flip_queries(2, operand_bank())
+        weigh(1, [0])
+        add_bias_to_head(0, 1, nc.vector)
+        row_maxima(0)
+        add_bias_to_head(1, 0, nc.gpsimd)
+        weigh(1, [1])
+        add_bias_to_head(1, 1, nc.gpsimd)
+        score_matmuls(2)
+        flip_queries(3, operand_bank())
+        exponentials(0)
+        for piece in range(VALUE_PIECES):
+            group_values(0, piece)
+        weigh(2)
+        score_matmuls(3)
+        flip_operands(0)
+        flip_probs(0)
+
         last = PAIRS - 1
-        for step in range(-QT, last - 1):
-            if live(step):
-                row_maxima(step)
-                exponentials(step)
-            if live(step - 1):
-                group_probs(step - 1)
+        for step in range(1, last - 1):
+            row_maxima(step)
+            exponentials(step)
+            group_probs(step - 1)
             if live(step - 3):
                 normalise_and_store(step - 3)
-            if live(step + 2):
-                weigh(step + 2)
+            weigh(step + 2)
             if live(step + SCORE_LEAD):
                 score_matmuls(step + SCORE_LEAD)
             flip_operands(step)
-            if step == -1:
-                for piece in range(VALUE_PIECES):
-                    group_values(0, piece)
-            elif step >= 0 and step % QT >= KEY_QUARTERS and step // QT + 1 < B:
+            if step % QT >= KEY_QUARTERS and step // QT + 1 < B:
                 group_values(step // QT + 1, step % QT - KEY_QUARTERS)
-            if live(step + 1):
-                add_bias(step + 1)
+            add_bias(step + 1)
             if live(step - 2):
                 invert_sums(step - 2)
                 if (step - 2) % QT == 0:
                     quantise_probs_and_values(step - 2)
                 else:
                     quantise_probs(step - 2)
-            if live(step):
-                flip_probs(step)
+            flip_probs(step)
             if live(step - 2):
                 product_bank(step - 2)
                 weighted_values(step - 2)
@@ -352,7 +392,7 @@ def tile_mistralselfattention_pb_t_kernel(tc, q_rot, k_rot, v, mask_w, mask_b, o
         exponentials(last)
         flip_probs(last, spare_banks=True)
         normalise_and_store(last - 4, on_vector=True)
-        for pair in range(last - 3, last + 1):
+        for pair in range(last - 3, last):
             invert_sums(pair)
         quantise_probs(last - 3)
         quantise_probs(last - 2)
@@ -368,6 +408,7 @@ def tile_mistralselfattention_pb_t_kernel(tc, q_rot, k_rot, v, mask_w, mask_b, o
         product_bank(last - 1, spare_bank=True)
         weighted_values(last - 1)
         product_bank(last)
+        invert_sums(last)
         for h in range(H):
             quantise_probs(last, h, 1)
             weighted_values(last, [h])

@@ -92,11 +92,11 @@ def tile_mistralselfattention_pb_t_kernel(tc, q_rot, k_rot, v, mask_w, mask_b, o
             nc.sync.dma_start(out=bias_rows[qt][:], in_=mask_b[0, 0, rows, :])
 
         load_keys(0, 0, QT // 2)
-        load_queries(0, 0, 1)
+        load_queries(0, 0, 2)
         load_keys(0, QT // 2, QT // 2)
         load_masks(0)
-        load_queries(0, 1, QT - 1)
         load_masks(1)
+        load_queries(0, 2, QT - 2)
         load_values(0)
         load_masks(2)
         load_keys(1)
@@ -165,9 +165,9 @@ def tile_mistralselfattention_pb_t_kernel(tc, q_rot, k_rot, v, mask_w, mask_b, o
                 out=v_grouped[b][:, :, columns, :], in_=v_raw[b][:, :, :, columns].rearrange("p g t d -> p g d t")
             )
 
-        def score_matmuls(pair):
+        def score_matmuls(pair, heads=range(H)):
             b, qt = divmod(pair, QT)
-            for h in range(H):
+            for h in heads:
                 for half in range(HALVES):
                     bank = score_banks.tile([P, BANK], F32, name="score_bank")
                     scores[(pair, h, half)] = bank
@@ -209,39 +209,37 @@ def tile_mistralselfattention_pb_t_kernel(tc, q_rot, k_rot, v, mask_w, mask_b, o
             scores_of_head = masked[pair][:, h, :]
             engine.tensor_tensor(out=scores_of_head, in0=scores_of_head, in1=bias_rows[pair % QT][:], op=ALU.add)
 
-        def row_maxima(pair, first=0, heads=H):
-            if first == 0:
+        def row_maxima(pair, h):
+            if h == 0:
                 neg_max[pair] = small.tile([P, H], F32, name="neg_max")
-            of_heads = slice(first, first + heads)
             nc.vector.tensor_reduce(
-                out=neg_max[pair][:, of_heads], in_=masked[pair][:, of_heads, :], axis=AXIS.X, op=ALU.max, negate=True
+                out=neg_max[pair][:, h : h + 1], in_=masked[pair][:, h, :], axis=AXIS.X, op=ALU.max, negate=True
             )
 
-        def exponentials(pair):
-            probs[pair] = work.tile([P, H, T], BF16, name="probs")
-            row_sum[pair] = small.tile([P, H], F32, name="row_sum")
-            for h in range(H):
-                nc.scalar.activation(
-                    out=probs[pair][:, h, :],
-                    in_=masked[pair][:, h, :],
-                    func=ACT.Exp,
-                    bias=neg_max[pair][:, h : h + 1],
-                    scale=1.0,
-                    accum_out=row_sum[pair][:, h : h + 1],
-                )
+        def exponentials(pair, h):
+            if h == 0:
+                probs[pair] = work.tile([P, H, T], BF16, name="probs")
+                row_sum[pair] = small.tile([P, H], F32, name="row_sum")
+            nc.scalar.activation(
+                out=probs[pair][:, h, :],
+                in_=masked[pair][:, h, :],
+                func=ACT.Exp,
+                bias=neg_max[pair][:, h : h + 1],
+                scale=1.0,
+                accum_out=row_sum[pair][:, h : h + 1],
+            )
 
-        def flip_probs(pair, spare_banks=False):
-            for h in range(H):
-                if spare_banks:
-                    bank = score_banks.tile([P, PASSES * 2, P], F32, name="spare_prob_bank", tag="score_bank")
-                else:
-                    bank = prob_banks.tile([P, PASSES * 2, P], F32, name="prob_bank")
-                probs_flipped[(pair, h)] = bank
-                words = probs[pair][:, h, :].bitcast(F32)
-                for g in range(PASSES):
-                    for u in range(2):
-                        first = g * 2 * P + u
-                        nc.tensor.transpose(bank[:, 2 * g + u, :], words[:, first : (g + 1) * 2 * P : 2], ident_f32[:])
+        def flip_probs(pair, h, spare_bank=False):
+            if spare_bank:
+                bank = score_banks.tile([P, PASSES * 2, P], F32, name="spare_prob_bank", tag="score_bank")
+            else:
+                bank = prob_banks.tile([P, PASSES * 2, P], F32, name="prob_bank")
+            probs_flipped[(pair, h)] = bank
+            words = probs[pair][:, h, :].bitcast(F32)
+            for g in range(PASSES):
+                for u in range(2):
+                    first = g * 2 * P + u
+                    nc.tensor.transpose(bank[:, 2 * g + u, :], words[:, first : (g + 1) * 2 * P : 2], ident_f32[:])
 
         def group_probs(pair, copy=nc.scalar.copy):
             if pair % QT == 0:
@@ -331,42 +329,53 @@ def tile_mistralselfattention_pb_t_kernel(tc, q_rot, k_rot, v, mask_w, mask_b, o
         flip_keys(0, 1, operand_bank(idle_score_bank=True), copy=nc.vector.tensor_copy)
         flip_queries(0, operand_bank(idle_score_bank=True))
         flip_keys(0, 2, operand_bank(idle_score_bank=True), copy=nc.vector.tensor_copy)
-        flip_keys(0, 3, operand_bank())
+        bank = operand_bank()
+        flip_keys(0, 3, bank)
+        flip_queries(1, bank)
 
         score_matmuls(0)
-        flip_queries(1, operand_bank())
+        flip_queries(2, operand_bank())
         weigh(0, [0])
         add_bias_to_head(0, 0, nc.gpsimd)
         weigh(0, [1])
         score_matmuls(1)
-        flip_queries(2, operand_bank())
+        flip_queries(3, operand_bank())
         weigh(1, [0])
         add_bias_to_head(0, 1, nc.vector)
-        row_maxima(0)
+        for h in range(H):
+            row_maxima(0, h)
         add_bias_to_head(1, 0, nc.gpsimd)
         weigh(1, [1])
         add_bias_to_head(1, 1, nc.gpsimd)
         score_matmuls(2)
-        flip_queries(3, operand_bank())
-        exponentials(0)
+        for h in range(H):
+            exponentials(0, h)
         for piece in range(VALUE_PIECES):
             group_values(0, piece)
         weigh(2)
         score_matmuls(3)
         flip_operands(0)
-        flip_probs(0)
+        for h in range(H):
+            flip_probs(0, h)
 
         last = PAIRS - 1
         for step in range(1, last - 1):
-            row_maxima(step)
-            exponentials(step)
+            row_maxima(step, 0)
+            exponentials(step, 0)
             group_probs(step - 1)
+            weigh(step + 2, [0])
+            if live(step + SCORE_LEAD):
+                score_matmuls(step + SCORE_LEAD, [0])
+            flip_probs(step, 0)
+            row_maxima(step, 1)
+            exponentials(step, 1)
             if live(step - 3):
                 normalise_and_store(step - 3)
-            weigh(step + 2)
-            if live(step + SCORE_LEAD):
-                score_matmuls(step + SCORE_LEAD)
+            weigh(step + 2, [1])
             flip_operands(step)
+            if live(step + SCORE_LEAD):
+                score_matmuls(step + SCORE_LEAD, [1])
+            flip_probs(step, 1)
             if step % QT >= KEY_QUARTERS and step // QT + 1 < B:
                 group_values(step // QT + 1, step % QT - KEY_QUARTERS)
             add_bias(step + 1)
@@ -376,26 +385,29 @@ def tile_mistralselfattention_pb_t_kernel(tc, q_rot, k_rot, v, mask_w, mask_b, o
                     quantise_probs_and_values(step - 2)
                 else:
                     quantise_probs(step - 2)
-            flip_probs(step)
             if live(step - 2):
                 product_bank(step - 2)
                 weighted_values(step - 2)
 
-        row_maxima(last - 1)
-        group_probs(last - 2)
-        add_bias_to_head(last, 0, nc.gpsimd)
-        add_bias_to_head(last, 1, nc.vector)
-        exponentials(last - 1)
-        flip_probs(last - 1)
         for h in range(H):
-            row_maxima(last, h, 1)
-        exponentials(last)
-        flip_probs(last, spare_banks=True)
-        normalise_and_store(last - 4, on_vector=True)
-        for pair in range(last - 3, last):
+            add_bias_to_head(last, h, nc.gpsimd)
+        for h in range(H):
+            row_maxima(last - 1, h)
+        group_probs(last - 2)
+        for h in range(H):
+            exponentials(last - 1, h)
+            flip_probs(last - 1, h)
+        for pair in range(last - 3, last - 1):
             invert_sums(pair)
+        row_maxima(last, 0)
+        normalise_and_store(last - 4, on_vector=True)
+        row_maxima(last, 1)
+        for h in range(H):
+            exponentials(last, h)
+            flip_probs(last, h, spare_bank=True)
         quantise_probs(last - 3)
         quantise_probs(last - 2)
+        invert_sums(last - 1)
         product_bank(last - 3)
         weighted_values(last - 3)
         product_bank(last - 2, spare_bank=True)

@@ -92,9 +92,10 @@ def tile_mistralselfattention_pb_t_kernel(tc, q_rot, k_rot, v, mask_w, mask_b, o
             nc.sync.dma_start(out=bias_rows[qt][:], in_=mask_b[0, 0, rows, :])
 
         load_keys(0, 0, QT // 2)
-        load_queries(0, 0, 2)
+        load_queries(0, 0, 1)
         load_keys(0, QT // 2, QT // 2)
         load_masks(0)
+        load_queries(0, 1, 1)
         load_masks(1)
         load_queries(0, 2, QT - 2)
         load_values(0)
@@ -110,7 +111,7 @@ def tile_mistralselfattention_pb_t_kernel(tc, q_rot, k_rot, v, mask_w, mask_b, o
             load_values(b)
 
         q_flipped, k_flipped, v_with_probs, v_grouped, v_codes, v_scales = {}, {}, {}, {}, {}, {}
-        scores, masked, neg_max, row_sum, inv_sum = {}, {}, {}, {}, {}
+        scores, masked, neg_max, row_sum, sums, inv_sum, inverses = {}, {}, {}, {}, {}, {}, {}
         probs, probs_flipped, probs_grouped, prob_codes, prob_scales, products, result = {}, {}, {}, {}, {}, {}, {}
 
         def live(pair):
@@ -210,16 +211,19 @@ def tile_mistralselfattention_pb_t_kernel(tc, q_rot, k_rot, v, mask_w, mask_b, o
             engine.tensor_tensor(out=scores_of_head, in0=scores_of_head, in1=bias_rows[pair % QT][:], op=ALU.add)
 
         def row_maxima(pair, h):
-            if h == 0:
+            if pair not in neg_max:
                 neg_max[pair] = small.tile([P, H], F32, name="neg_max")
             nc.vector.tensor_reduce(
                 out=neg_max[pair][:, h : h + 1], in_=masked[pair][:, h, :], axis=AXIS.X, op=ALU.max, negate=True
             )
 
         def exponentials(pair, h):
-            if h == 0:
+            if pair not in probs:
                 probs[pair] = work.tile([P, H, T], BF16, name="probs")
-                row_sum[pair] = small.tile([P, H], F32, name="row_sum")
+                if pair % 2 == 0:
+                    sums_of_two = small.tile([P, 2 * H], F32, name="row_sums")
+                    row_sum[pair], row_sum[pair + 1] = sums_of_two[:, 0:H], sums_of_two[:, H : 2 * H]
+                    sums[pair] = sums_of_two
             nc.scalar.activation(
                 out=probs[pair][:, h, :],
                 in_=masked[pair][:, h, :],
@@ -241,20 +245,26 @@ def tile_mistralselfattention_pb_t_kernel(tc, q_rot, k_rot, v, mask_w, mask_b, o
                     first = g * 2 * P + u
                     nc.tensor.transpose(bank[:, 2 * g + u, :], words[:, first : (g + 1) * 2 * P : 2], ident_f32[:])
 
-        def group_probs(pair, copy=nc.scalar.copy):
+        def group_probs(pair, copy=nc.scalar.copy, heads=range(H)):
             if pair % QT == 0:
                 probs_grouped[pair] = v_with_probs[pair // QT][:, 0].rearrange("p (h n) -> p h n", h=H)
             else:
                 probs_grouped[pair] = work.tile([P, H, T], BF16, name="probs_grouped", align_bytes=64)[:]
-            for h in range(H):
+            for h in heads:
                 copy(
                     out=probs_grouped[pair][:, h].bitcast(F32).rearrange("p (g q u) -> p g q u", g=PASSES, u=2),
                     in_=probs_flipped[(pair, h)][:].rearrange("p (g u) q -> p g q u", u=2),
                 )
 
-        def invert_sums(pair):
-            inv_sum[pair] = small.tile([P, H], F32, name="inv_sum")
-            nc.vector.reciprocal(out=inv_sum[pair][:], in_=row_sum[pair][:])
+        def invert_sums(pair, pairs=1):
+            if pair % 2 == 0:
+                inverses_of_two = small.tile([P, 2 * H], F32, name="inverses")
+                inv_sum[pair], inv_sum[pair + 1] = inverses_of_two[:, 0:H], inverses_of_two[:, H : 2 * H]
+                inverses[pair] = inverses_of_two
+            first = pair % 2 * H
+            columns = slice(first, first + pairs * H)
+            even = pair - pair % 2
+            nc.vector.reciprocal(out=inverses[even][:, columns], in_=sums[even][:, columns])
 
         def quantise(codes, scales, values):
             nc.vector.quantize_mx(out=codes.bitcast(FP8X4), scales=scales, in_=values)
@@ -272,7 +282,7 @@ def tile_mistralselfattention_pb_t_kernel(tc, q_rot, k_rot, v, mask_w, mask_b, o
             v_codes[b], v_scales[b] = codes[:, 1], scales[:, 1]
 
         def quantise_probs(pair, first=0, heads=H):
-            if first == 0:
+            if pair not in prob_codes:
                 prob_codes[pair] = work.tile([P, WORDS], U32, name="prob_codes", align_bytes=64)[:]
                 prob_scales[pair] = work.tile([P, WORDS], U8, name="prob_scales", align_bytes=64)[:]
             words = slice(first * WORDS // H, (first + heads) * WORDS // H)
@@ -306,7 +316,7 @@ def tile_mistralselfattention_pb_t_kernel(tc, q_rot, k_rot, v, mask_w, mask_b, o
                     )
 
         def normalise(pair, h, on_vector=False):
-            if h == 0:
+            if pair not in result:
                 result[pair] = result_pool.tile([P, H, D], F32, name="result")
             factor = inv_sum[pair][:, h : h + 1]
             if on_vector:
@@ -329,11 +339,11 @@ def tile_mistralselfattention_pb_t_kernel(tc, q_rot, k_rot, v, mask_w, mask_b, o
         flip_keys(0, 1, operand_bank(idle_score_bank=True), copy=nc.vector.tensor_copy)
         flip_queries(0, operand_bank(idle_score_bank=True))
         flip_keys(0, 2, operand_bank(idle_score_bank=True), copy=nc.vector.tensor_copy)
-        bank = operand_bank()
-        flip_keys(0, 3, bank)
-        flip_queries(1, bank)
+        flip_keys(0, 3, operand_bank())
 
-        score_matmuls(0)
+        score_matmuls(0, [0])
+        flip_queries(1, operand_bank())
+        score_matmuls(0, [1])
         flip_queries(2, operand_bank())
         weigh(0, [0])
         add_bias_to_head(0, 0, nc.gpsimd)
@@ -371,6 +381,8 @@ def tile_mistralselfattention_pb_t_kernel(tc, q_rot, k_rot, v, mask_w, mask_b, o
             exponentials(step, 1)
             if live(step - 3):
                 normalise_and_store(step - 3)
+            if step % 2 == 0:
+                invert_sums(step - 2, pairs=2)
             weigh(step + 2, [1])
             flip_operands(step)
             if live(step + SCORE_LEAD):
@@ -380,7 +392,6 @@ def tile_mistralselfattention_pb_t_kernel(tc, q_rot, k_rot, v, mask_w, mask_b, o
                 group_values(step // QT + 1, step % QT - KEY_QUARTERS)
             add_bias(step + 1)
             if live(step - 2):
-                invert_sums(step - 2)
                 if (step - 2) % QT == 0:
                     quantise_probs_and_values(step - 2)
                 else:
@@ -389,7 +400,7 @@ def tile_mistralselfattention_pb_t_kernel(tc, q_rot, k_rot, v, mask_w, mask_b, o
                 product_bank(step - 2)
                 weighted_values(step - 2)
 
-        for h in range(H):
+        for h in reversed(range(H)):
             add_bias_to_head(last, h, nc.gpsimd)
         for h in range(H):
             row_maxima(last - 1, h)
@@ -397,12 +408,11 @@ def tile_mistralselfattention_pb_t_kernel(tc, q_rot, k_rot, v, mask_w, mask_b, o
         for h in range(H):
             exponentials(last - 1, h)
             flip_probs(last - 1, h)
-        for pair in range(last - 3, last - 1):
-            invert_sums(pair)
-        row_maxima(last, 0)
-        normalise_and_store(last - 4, on_vector=True)
+        invert_sums(last - 3, pairs=2)
         row_maxima(last, 1)
-        for h in range(H):
+        normalise_and_store(last - 4, on_vector=True)
+        row_maxima(last, 0)
+        for h in reversed(range(H)):
             exponentials(last, h)
             flip_probs(last, h, spare_bank=True)
         quantise_probs(last - 3)
@@ -413,7 +423,7 @@ def tile_mistralselfattention_pb_t_kernel(tc, q_rot, k_rot, v, mask_w, mask_b, o
         product_bank(last - 2, spare_bank=True)
         weighted_values(last - 2)
         group_probs(last - 1, copy=nc.vector.tensor_copy)
-        group_probs(last)
+        group_probs(last, heads=[1, 0])
         normalise_and_store(last - 3)
         normalise_and_store(last - 2)
         quantise_probs(last - 1)
@@ -421,10 +431,10 @@ def tile_mistralselfattention_pb_t_kernel(tc, q_rot, k_rot, v, mask_w, mask_b, o
         weighted_values(last - 1)
         product_bank(last)
         invert_sums(last)
-        for h in range(H):
+        for h in reversed(range(H)):
             quantise_probs(last, h, 1)
             weighted_values(last, [h])
         normalise_and_store(last - 1)
-        normalise(last, 0)
-        normalise(last, 1, on_vector=True)
+        normalise(last, 1)
+        normalise(last, 0, on_vector=True)
         store(last)

@@ -41,7 +41,7 @@ def tile_mistralselfattention_pb_t_kernel(tc, q_rot, k_rot, v, mask_w, mask_b, o
         flipped_pool = ctx.enter_context(tc.tile_pool(name="flipped", bufs=2))
         value_pool = ctx.enter_context(tc.tile_pool(name="values", bufs=2))
         masked_pool = ctx.enter_context(tc.tile_pool(name="masked", bufs=3))
-        work = ctx.enter_context(tc.tile_pool(name="work", bufs=2))
+        work = ctx.enter_context(tc.tile_pool(name="work", bufs=3))
         small = ctx.enter_context(tc.tile_pool(name="small", bufs=4))
         result_pool = ctx.enter_context(tc.tile_pool(name="result", bufs=6))
         score_banks = ctx.enter_context(tc.psum_pool(name="score_banks", bufs=H * HALVES))
@@ -122,24 +122,29 @@ def tile_mistralselfattention_pb_t_kernel(tc, q_rot, k_rot, v, mask_w, mask_b, o
                 return score_banks.tile([P, 2, DC, 2, P], BF16, name="early_operand_bank", tag="score_bank")
             return operand_banks.tile([P, 2, DC, 2, P], BF16, name="operand_bank")
 
-        def flip_queries(pair, bank, copy=nc.scalar.copy):
+        def transpose_queries(pair, bank):
             b, qt = divmod(pair, QT)
-            if qt == 0:
-                q_flipped[b] = flipped_pool.tile([P, DC, H, T], BF16, name="q_flipped")
             for c in range(DC):
                 for h in range(H):
                     first = h * D + c * P
                     nc.tensor.transpose(bank[:, 0, c, h, :], q_raw[b][:, qt, first : first + P], ident_bf16[:])
+
+        def copy_queries(pair, bank, copy=nc.scalar.copy):
+            b, qt = divmod(pair, QT)
+            if qt == 0:
+                q_flipped[b] = flipped_pool.tile([P, DC, H, T], BF16, name="q_flipped")
             copy(out=q_flipped[b][:, :, :, qt * P : (qt + 1) * P], in_=bank[:, 0])
 
-        def flip_keys(b, quarter, bank, copy=nc.scalar.copy):
-            if quarter == 0:
-                k_flipped[b] = flipped_pool.tile([P, DC, T], BF16, name="k_flipped")
+        def transpose_keys(b, quarter, bank):
             for c in range(DC):
                 for j in range(2):
                     nc.tensor.transpose(
                         bank[:, 1, c, j, :], k_raw[b][:, 2 * quarter + j, c * P : (c + 1) * P], ident_bf16[:]
                     )
+
+        def copy_keys(b, quarter, bank, copy=nc.scalar.copy):
+            if quarter == 0:
+                k_flipped[b] = flipped_pool.tile([P, DC, T], BF16, name="k_flipped")
             copy(
                 out=k_flipped[b][:, :, 2 * quarter * P : 2 * (quarter + 1) * P],
                 in_=bank[:, 1].rearrange("p c j k -> p c (j k)"),
@@ -152,9 +157,21 @@ def tile_mistralselfattention_pb_t_kernel(tc, q_rot, k_rot, v, mask_w, mask_b, o
             if live(pair) or with_keys:
                 bank = operand_bank()
             if live(pair):
-                flip_queries(pair, bank)
+                transpose_queries(pair, bank)
             if with_keys:
-                flip_keys(next_b, quarter, bank)
+                transpose_keys(next_b, quarter, bank)
+            if live(pair):
+                copy_queries(pair, bank)
+            if with_keys:
+                copy_keys(next_b, quarter, bank)
+
+        def flip_queries(pair, bank, copy=nc.scalar.copy):
+            transpose_queries(pair, bank)
+            copy_queries(pair, bank, copy)
+
+        def flip_keys(b, quarter, bank, copy=nc.scalar.copy):
+            transpose_keys(b, quarter, bank)
+            copy_keys(b, quarter, bank, copy)
 
         def group_values(b, piece):
             if piece == 0:
@@ -248,7 +265,7 @@ def tile_mistralselfattention_pb_t_kernel(tc, q_rot, k_rot, v, mask_w, mask_b, o
         def group_probs(pair, copy=nc.scalar.copy, heads=range(H)):
             if pair % QT == 0:
                 probs_grouped[pair] = v_with_probs[pair // QT][:, 0].rearrange("p (h n) -> p h n", h=H)
-            else:
+            elif pair not in probs_grouped:
                 probs_grouped[pair] = work.tile([P, H, T], BF16, name="probs_grouped", align_bytes=64)[:]
             for h in heads:
                 copy(
@@ -412,25 +429,27 @@ def tile_mistralselfattention_pb_t_kernel(tc, q_rot, k_rot, v, mask_w, mask_b, o
         row_maxima(last, 1)
         normalise_and_store(last - 4, on_vector=True)
         row_maxima(last, 0)
-        for h in reversed(range(H)):
-            exponentials(last, h)
-            flip_probs(last, h, spare_bank=True)
+        exponentials(last, 1)
+        flip_probs(last, 1, spare_bank=True)
+        exponentials(last, 0)
         quantise_probs(last - 3)
-        quantise_probs(last - 2)
-        invert_sums(last - 1)
         product_bank(last - 3)
         weighted_values(last - 3)
+        flip_probs(last, 0, spare_bank=True)
+        quantise_probs(last - 2)
         product_bank(last - 2, spare_bank=True)
         weighted_values(last - 2)
+        invert_sums(last - 1)
         group_probs(last - 1, copy=nc.vector.tensor_copy)
-        group_probs(last, heads=[1, 0])
+        group_probs(last, heads=[1])
         normalise_and_store(last - 3)
-        normalise_and_store(last - 2)
+        group_probs(last, heads=[0])
         quantise_probs(last - 1)
         product_bank(last - 1, spare_bank=True)
         weighted_values(last - 1)
-        product_bank(last)
+        normalise_and_store(last - 2)
         invert_sums(last)
+        product_bank(last)
         for h in reversed(range(H)):
             quantise_probs(last, h, 1)
             weighted_values(last, [h])

@@ -23,6 +23,7 @@ WORDS = H * T // PACK
 HALVES = T // BANK
 PAIRS = B * QT
 SCORE_SCALE = 1.0 / 16.0
+WARM_UP = 3
 KEY_QUARTERS = 4
 VALUE_PIECES = 4
 QUERY_LEAD = 4
@@ -59,6 +60,12 @@ def tile_mistralselfattention_pb_t_kernel(tc, q_rot, k_rot, v, mask_w, mask_b, o
         one = const.tile([P, 1], F32)
         nc.scalar.activation(out=one[:], in_=zero[:], func=ACT.Exp)
 
+        zeros = const.tile([P, BANK], BF16)
+        nc.vector.memset(zeros[:], 0.0)
+        idle_bank = out_banks.tile([P, BANK], F32, name="idle_bank", tag="out_bank")
+        for turn in range(WARM_UP):
+            nc.tensor.matmul(out=idle_bank[:], lhsT=zeros[:, 0:P], rhs=zeros[:], start=True, stop=True)
+
         q_raw, k_raw, v_raw, weight_rows, bias_rows = {}, {}, {}, {}, {}
 
         def load_keys(b, first=0, tiles=QT):
@@ -84,18 +91,24 @@ def tile_mistralselfattention_pb_t_kernel(tc, q_rot, k_rot, v, mask_w, mask_b, o
                 in_=v[b].rearrange("(g p t) o d -> p g (t o d)", p=P, t=PACK),
             )
 
-        def load_masks(qt):
-            rows = slice(qt * P, (qt + 1) * P)
+        def load_weights(qt):
             weight_rows[qt] = mask_pool.tile([P, T], BF16, name="weight_rows%d" % qt)
-            nc.sync.dma_start(out=weight_rows[qt][:], in_=mask_w[0, 0, rows, :])
+            nc.sync.dma_start(out=weight_rows[qt][:], in_=mask_w[0, 0, qt * P : (qt + 1) * P, :])
+
+        def load_biases(qt):
             bias_rows[qt] = mask_pool.tile([P, T], BF16, name="bias_rows%d" % qt)
-            nc.sync.dma_start(out=bias_rows[qt][:], in_=mask_b[0, 0, rows, :])
+            nc.sync.dma_start(out=bias_rows[qt][:], in_=mask_b[0, 0, qt * P : (qt + 1) * P, :])
+
+        def load_masks(qt):
+            load_weights(qt)
+            load_biases(qt)
 
         load_keys(0, 0, QT // 2)
         load_queries(0, 0, 1)
         load_keys(0, QT // 2, QT // 2)
-        load_masks(0)
+        load_weights(0)
         load_queries(0, 1, 1)
+        load_biases(0)
         load_masks(1)
         load_queries(0, 2, QT - 2)
         load_values(0)
@@ -122,32 +135,32 @@ def tile_mistralselfattention_pb_t_kernel(tc, q_rot, k_rot, v, mask_w, mask_b, o
                 return score_banks.tile([P, 2, DC, 2, P], BF16, name="early_operand_bank", tag="score_bank")
             return operand_banks.tile([P, 2, DC, 2, P], BF16, name="operand_bank")
 
-        def transpose_queries(pair, bank):
+        def transpose_queries(pair, half):
             b, qt = divmod(pair, QT)
             for c in range(DC):
                 for h in range(H):
                     first = h * D + c * P
-                    nc.tensor.transpose(bank[:, 0, c, h, :], q_raw[b][:, qt, first : first + P], ident_bf16[:])
+                    nc.tensor.transpose(half[:, c, h, :], q_raw[b][:, qt, first : first + P], ident_bf16[:])
 
-        def copy_queries(pair, bank, copy=nc.scalar.copy):
+        def copy_queries(pair, half, copy=nc.scalar.copy):
             b, qt = divmod(pair, QT)
             if qt == 0:
                 q_flipped[b] = flipped_pool.tile([P, DC, H, T], BF16, name="q_flipped")
-            copy(out=q_flipped[b][:, :, :, qt * P : (qt + 1) * P], in_=bank[:, 0])
+            copy(out=q_flipped[b][:, :, :, qt * P : (qt + 1) * P], in_=half)
 
-        def transpose_keys(b, quarter, bank):
+        def transpose_keys(b, quarter, half):
             for c in range(DC):
                 for j in range(2):
                     nc.tensor.transpose(
-                        bank[:, 1, c, j, :], k_raw[b][:, 2 * quarter + j, c * P : (c + 1) * P], ident_bf16[:]
+                        half[:, c, j, :], k_raw[b][:, 2 * quarter + j, c * P : (c + 1) * P], ident_bf16[:]
                     )
 
-        def copy_keys(b, quarter, bank, copy=nc.scalar.copy):
+        def copy_keys(b, quarter, half, copy=nc.scalar.copy):
             if quarter == 0:
                 k_flipped[b] = flipped_pool.tile([P, DC, T], BF16, name="k_flipped")
             copy(
                 out=k_flipped[b][:, :, 2 * quarter * P : 2 * (quarter + 1) * P],
-                in_=bank[:, 1].rearrange("p c j k -> p c (j k)"),
+                in_=half.rearrange("p c j k -> p c (j k)"),
             )
 
         def flip_operands(step):
@@ -157,21 +170,21 @@ def tile_mistralselfattention_pb_t_kernel(tc, q_rot, k_rot, v, mask_w, mask_b, o
             if live(pair) or with_keys:
                 bank = operand_bank()
             if live(pair):
-                transpose_queries(pair, bank)
+                transpose_queries(pair, bank[:, 0])
             if with_keys:
-                transpose_keys(next_b, quarter, bank)
+                transpose_keys(next_b, quarter, bank[:, 1])
             if live(pair):
-                copy_queries(pair, bank)
+                copy_queries(pair, bank[:, 0])
             if with_keys:
-                copy_keys(next_b, quarter, bank)
+                copy_keys(next_b, quarter, bank[:, 1])
 
         def flip_queries(pair, bank, copy=nc.scalar.copy):
-            transpose_queries(pair, bank)
-            copy_queries(pair, bank, copy)
+            transpose_queries(pair, bank[:, 0])
+            copy_queries(pair, bank[:, 0], copy)
 
         def flip_keys(b, quarter, bank, copy=nc.scalar.copy):
-            transpose_keys(b, quarter, bank)
-            copy_keys(b, quarter, bank, copy)
+            transpose_keys(b, quarter, bank[:, 0])
+            copy_keys(b, quarter, bank[:, 0], copy)
 
         def group_values(b, piece):
             if piece == 0:
@@ -242,8 +255,8 @@ def tile_mistralselfattention_pb_t_kernel(tc, q_rot, k_rot, v, mask_w, mask_b, o
                     row_sum[pair], row_sum[pair + 1] = sums_of_two[:, 0:H], sums_of_two[:, H : 2 * H]
                     sums[pair] = sums_of_two
             nc.scalar.activation(
-                out=probs[pair][:, h, :],
-                in_=masked[pair][:, h, :],
+                out=probs[pair][:, h, :].rearrange("p (u w e) -> p u w e", u=2, e=2),
+                in_=masked[pair][:, h, :].rearrange("p (w u e) -> p u w e", u=2, e=2),
                 func=ACT.Exp,
                 bias=neg_max[pair][:, h : h + 1],
                 scale=1.0,
@@ -259,8 +272,8 @@ def tile_mistralselfattention_pb_t_kernel(tc, q_rot, k_rot, v, mask_w, mask_b, o
             words = probs[pair][:, h, :].bitcast(F32)
             for g in range(PASSES):
                 for u in range(2):
-                    first = g * 2 * P + u
-                    nc.tensor.transpose(bank[:, 2 * g + u, :], words[:, first : (g + 1) * 2 * P : 2], ident_f32[:])
+                    first = (u * PASSES + g) * P
+                    nc.tensor.transpose(bank[:, 2 * g + u, :], words[:, first : first + P], ident_f32[:])
 
         def group_probs(pair, copy=nc.scalar.copy, heads=range(H)):
             if pair % QT == 0:
@@ -361,12 +374,15 @@ def tile_mistralselfattention_pb_t_kernel(tc, q_rot, k_rot, v, mask_w, mask_b, o
         score_matmuls(0, [0])
         flip_queries(1, operand_bank())
         score_matmuls(0, [1])
-        flip_queries(2, operand_bank())
         weigh(0, [0])
         add_bias_to_head(0, 0, nc.gpsimd)
         weigh(0, [1])
         score_matmuls(1)
-        flip_queries(3, operand_bank())
+        bank = operand_bank()
+        for i in range(2):
+            transpose_queries(2 + i, bank[:, i])
+        for i in range(2):
+            copy_queries(2 + i, bank[:, i])
         weigh(1, [0])
         add_bias_to_head(0, 1, nc.vector)
         for h in range(H):

from contextlib import ExitStack

import concourse.masks as masks
import concourse.mybir as mybir

F32 = mybir.dt.float32
BF16 = mybir.dt.bfloat16
U32 = mybir.dt.uint32
U8 = mybir.dt.uint8
FP8X4 = mybir.dt.float8_e4m3fn_x4
ALU = mybir.AluOpType
ACT = mybir.ActivationFunctionType
AXIS = mybir.AxisListType

B, T, H, D = 4, 1024, 2, 256
P = 128
BANK = 512
PACK = 4
PASSES = T // (P * PACK)
QT = T // P
DC = D // P
WORDS = H * T // PACK
HALVES = T // BANK
PAIRS = B * QT
SCORE_SCALE = 1.0 / 16.0
WARM_UP = 3
KEY_QUARTERS = 4
VALUE_PIECES = 4
QUERY_LEAD = 4
SCORE_LEAD = 3

FLOPS = 2 * 2 * B * H * T * T * D


def tile_mistralselfattention_pb_t_kernel(tc, q_rot, k_rot, v, mask_w, mask_b, out):
    nc = tc.nc
    with ExitStack() as ctx:
        ctx.enter_context(tc.manual_schedule())
        const = ctx.enter_context(tc.tile_pool(name="const", bufs=1))
        mask_pool = ctx.enter_context(tc.tile_pool(name="masks", bufs=1))
        raw = ctx.enter_context(tc.tile_pool(name="raw", bufs=B))
        flipped_pool = ctx.enter_context(tc.tile_pool(name="flipped", bufs=2))
        value_pool = ctx.enter_context(tc.tile_pool(name="values", bufs=2))
        masked_pool = ctx.enter_context(tc.tile_pool(name="masked", bufs=3))
        work = ctx.enter_context(tc.tile_pool(name="work", bufs=3))
        small = ctx.enter_context(tc.tile_pool(name="small", bufs=4))
        result_pool = ctx.enter_context(tc.tile_pool(name="result", bufs=6))
        score_banks = ctx.enter_context(tc.psum_pool(name="score_banks", bufs=H * HALVES))
        prob_banks = ctx.enter_context(tc.psum_pool(name="prob_banks", bufs=H))
        out_banks = ctx.enter_context(tc.psum_pool(name="out_banks", bufs=1))
        operand_banks = ctx.enter_context(tc.psum_pool(name="operand_banks", bufs=1))

        ident_bf16 = const.tile([P, P], BF16)
        masks.make_identity(nc, ident_bf16[:])
        ident_f32 = const.tile([P, P], F32)
        masks.make_identity(nc, ident_f32[:])

        zero = const.tile([P, 1], F32)
        nc.vector.memset(zero[:], 0.0)
        one = const.tile([P, 1], F32)
        nc.scalar.activation(out=one[:], in_=zero[:], func=ACT.Exp)

        zeros = const.tile([P, BANK], BF16)
        nc.vector.memset(zeros[:], 0.0)
        idle_bank = out_banks.tile([P, BANK], F32, name="idle_bank", tag="out_bank")
        for turn in range(WARM_UP):
            nc.tensor.matmul(out=idle_bank[:], lhsT=zeros[:, 0:P], rhs=zeros[:], start=True, stop=True)

        q_raw, k_raw, v_raw, weight_rows, bias_rows = {}, {}, {}, {}, {}

        def load_keys(b, first=0, tiles=QT):
            if first == 0:
                k_raw[b] = raw.tile([P, QT, D], BF16, name="k_raw")
            nc.sync.dma_start(
                out=k_raw[b][:, first : first + tiles, :],
                in_=k_rot[b, first * P : (first + tiles) * P].rearrange("(t p) o d -> p t (o d)", p=P),
            )

        def load_queries(b, first=0, tiles=QT):
            if first == 0:
                q_raw[b] = raw.tile([P, QT, H * D], BF16, name="q_raw")
            nc.sync.dma_start(
                out=q_raw[b][:, first : first + tiles, :],
                in_=q_rot[b, first * P : (first + tiles) * P].rearrange("(t p) h d -> p t (h d)", p=P),
            )

        def load_values(b):
            v_raw[b] = raw.tile([P, PASSES, PACK, D], BF16, name="v_raw")
            nc.sync.dma_start(
                out=v_raw[b][:].rearrange("p g t d -> p g (t d)"),
                in_=v[b].rearrange("(g p t) o d -> p g (t o d)", p=P, t=PACK),
            )

        def load_weights(qt):
            weight_rows[qt] = mask_pool.tile([P, T], BF16, name="weight_rows%d" % qt)
            nc.sync.dma_start(out=weight_rows[qt][:], in_=mask_w[0, 0, qt * P : (qt + 1) * P, :])

        def load_biases(qt):
            bias_rows[qt] = mask_pool.tile([P, T], BF16, name="bias_rows%d" % qt)
            nc.sync.dma_start(out=bias_rows[qt][:], in_=mask_b[0, 0, qt * P : (qt + 1) * P, :])

        def load_masks(qt):
            load_weights(qt)
            load_biases(qt)

        load_keys(0, 0, QT // 2)
        load_queries(0, 0, 1)
        load_keys(0, QT // 2, QT // 2)
        load_weights(0)
        load_queries(0, 1, 1)
        load_biases(0)
        load_masks(1)
        load_queries(0, 2, QT - 2)
        load_values(0)
        load_masks(2)
        load_keys(1)
        for qt in range(3, QT):
            load_masks(qt)
        load_queries(1)
        load_values(1)
        for b in range(2, B):
            load_keys(b)
            load_queries(b)
            load_values(b)

        q_flipped, k_flipped, v_with_probs, v_grouped, v_codes, v_scales = {}, {}, {}, {}, {}, {}
        scores, masked, neg_max, row_sum, sums, inv_sum, inverses = {}, {}, {}, {}, {}, {}, {}
        probs, probs_flipped, probs_grouped, prob_codes, prob_scales, products, result = {}, {}, {}, {}, {}, {}, {}

        def live(pair):
            return 0 <= pair < PAIRS

        def operand_bank(idle_score_bank=False):
            if idle_score_bank:
                return score_banks.tile([P, 2, DC, 2, P], BF16, name="early_operand_bank", tag="score_bank")
            return operand_banks.tile([P, 2, DC, 2, P], BF16, name="operand_bank")

        def transpose_queries(pair, half):
            b, qt = divmod(pair, QT)
            for c in range(DC):
                for h in range(H):
                    first = h * D + c * P
                    nc.tensor.transpose(half[:, c, h, :], q_raw[b][:, qt, first : first + P], ident_bf16[:])

        def copy_queries(pair, half, copy=nc.scalar.copy):
            b, qt = divmod(pair, QT)
            if qt == 0:
                q_flipped[b] = flipped_pool.tile([P, DC, H, T], BF16, name="q_flipped")
            copy(out=q_flipped[b][:, :, :, qt * P : (qt + 1) * P], in_=half)

        def transpose_keys(b, quarter, half):
            for c in range(DC):
                for j in range(2):
                    nc.tensor.transpose(
                        half[:, c, j, :], k_raw[b][:, 2 * quarter + j, c * P : (c + 1) * P], ident_bf16[:]
                    )

        def copy_keys(b, quarter, half, copy=nc.scalar.copy):
            if quarter == 0:
                k_flipped[b] = flipped_pool.tile([P, DC, T], BF16, name="k_flipped")
            copy(
                out=k_flipped[b][:, :, 2 * quarter * P : 2 * (quarter + 1) * P],
                in_=half.rearrange("p c j k -> p c (j k)"),
            )

        def flip_operands(step):
            pair = step + QUERY_LEAD
            next_b, quarter = step // QT + 1, step % QT
            with_keys = quarter < KEY_QUARTERS and next_b < B
            if live(pair) or with_keys:
                bank = operand_bank()
            if live(pair):
                transpose_queries(pair, bank[:, 0])
            if with_keys:
                transpose_keys(next_b, quarter, bank[:, 1])
            if live(pair):
                copy_queries(pair, bank[:, 0])
            if with_keys:
                copy_keys(next_b, quarter, bank[:, 1])

        def flip_queries(pair, bank, copy=nc.scalar.copy):
            transpose_queries(pair, bank[:, 0])
            copy_queries(pair, bank[:, 0], copy)

        def flip_keys(b, quarter, bank, copy=nc.scalar.copy):
            transpose_keys(b, quarter, bank[:, 0])
            copy_keys(b, quarter, bank[:, 0], copy)

        def group_values(b, piece):
            if piece == 0:
                v_with_probs[b] = value_pool.tile([P, 2, T * H], BF16, name="v_with_probs", align_bytes=64)
                v_grouped[b] = v_with_probs[b][:, 1].rearrange("p (g d t) -> p g d t", g=PASSES, t=PACK)
            width = D // VALUE_PIECES
            columns = slice(piece * width, (piece + 1) * width)
            nc.scalar.copy(
                out=v_grouped[b][:, :, columns, :], in_=v_raw[b][:, :, :, columns].rearrange("p g t d -> p g d t")
            )

        def score_matmuls(pair, heads=range(H)):
            b, qt = divmod(pair, QT)
            for h in heads:
                for half in range(HALVES):
                    bank = score_banks.tile([P, BANK], F32, name="score_bank")
                    scores[(pair, h, half)] = bank
                    for c in range(DC):
                        nc.tensor.matmul(
                            out=bank[:],
                            lhsT=q_flipped[b][:, c, h, qt * P : (qt + 1) * P],
                            rhs=k_flipped[b][:, c, half * BANK : (half + 1) * BANK],
                            start=(c == 0),
                            stop=(c == DC - 1),
                        )

        def weigh(pair, heads=range(H)):
            qt = pair % QT
            if 0 in heads:
                masked[pair] = masked_pool.tile([P, H, T], F32, name="masked")
            for h in heads:
                for half in range(HALVES):
                    keys = slice(half * BANK, (half + 1) * BANK)
                    nc.vector.scalar_tensor_tensor(
                        out=masked[pair][:, h, keys],
                        in0=scores[(pair, h, half)][:],
                        scalar=SCORE_SCALE,
                        in1=weight_rows[qt][:, keys],
                        op0=ALU.mult,
                        op1=ALU.mult,
                    )

        def add_bias(pair):
            qt = pair % QT
            nc.gpsimd.tensor_tensor(
                out=masked[pair][:],
                in0=masked[pair][:],
                in1=bias_rows[qt][:].unsqueeze(1).to_broadcast([P, H, T]),
                op=ALU.add,
            )

        def add_bias_to_head(pair, h, engine):
            scores_of_head = masked[pair][:, h, :]
            engine.tensor_tensor(out=scores_of_head, in0=scores_of_head, in1=bias_rows[pair % QT][:], op=ALU.add)

        def row_maxima(pair, h):
            if pair not in neg_max:
                neg_max[pair] = small.tile([P, H], F32, name="neg_max")
            nc.vector.tensor_reduce(
                out=neg_max[pair][:, h : h + 1], in_=masked[pair][:, h, :], axis=AXIS.X, op=ALU.max, negate=True
            )

        def exponentials(pair, h):
            if pair not in probs:
                probs[pair] = work.tile([P, H, T], BF16, name="probs")
                if pair % 2 == 0:
                    sums_of_two = small.tile([P, 2 * H], F32, name="row_sums")
                    row_sum[pair], row_sum[pair + 1] = sums_of_two[:, 0:H], sums_of_two[:, H : 2 * H]
                    sums[pair] = sums_of_two
            nc.scalar.activation(
                out=probs[pair][:, h, :].rearrange("p (u w e) -> p u w e", u=2, e=2),
                in_=masked[pair][:, h, :].rearrange("p (w u e) -> p u w e", u=2, e=2),
                func=ACT.Exp,
                bias=neg_max[pair][:, h : h + 1],
                scale=1.0,
                accum_out=row_sum[pair][:, h : h + 1],
            )

        def flip_probs(pair, h, spare_bank=False):
            if spare_bank:
                bank = score_banks.tile([P, PASSES * 2, P], F32, name="spare_prob_bank", tag="score_bank")
            else:
                bank = prob_banks.tile([P, PASSES * 2, P], F32, name="prob_bank")
            probs_flipped[(pair, h)] = bank
            words = probs[pair][:, h, :].bitcast(F32)
            for g in range(PASSES):
                for u in range(2):
                    first = (u * PASSES + g) * P
                    nc.tensor.transpose(bank[:, 2 * g + u, :], words[:, first : first + P], ident_f32[:])

        def group_probs(pair, copy=nc.scalar.copy, heads=range(H)):
            if pair % QT == 0:
                probs_grouped[pair] = v_with_probs[pair // QT][:, 0].rearrange("p (h n) -> p h n", h=H)
            elif pair not in probs_grouped:
                probs_grouped[pair] = work.tile([P, H, T], BF16, name="probs_grouped", align_bytes=64)[:]
            for h in heads:
                copy(
                    out=probs_grouped[pair][:, h].bitcast(F32).rearrange("p (g q u) -> p g q u", g=PASSES, u=2),
                    in_=probs_flipped[(pair, h)][:].rearrange("p (g u) q -> p g q u", u=2),
                )

        def invert_sums(pair, pairs=1):
            if pair % 2 == 0:
                inverses_of_two = small.tile([P, 2 * H], F32, name="inverses")
                inv_sum[pair], inv_sum[pair + 1] = inverses_of_two[:, 0:H], inverses_of_two[:, H : 2 * H]
                inverses[pair] = inverses_of_two
            first = pair % 2 * H
            columns = slice(first, first + pairs * H)
            even = pair - pair % 2
            nc.vector.reciprocal(out=inverses[even][:, columns], in_=sums[even][:, columns])

        def quantise(codes, scales, values):
            nc.vector.quantize_mx(out=codes.bitcast(FP8X4), scales=scales, in_=values)

        def quantise_probs_and_values(pair):
            b = pair // QT
            codes = value_pool.tile([P, 2, WORDS], U32, name="codes_with_v", align_bytes=64)
            scales = value_pool.tile([P, 2, WORDS], U8, name="scales_with_v", align_bytes=64)
            quantise(
                codes[:].rearrange("p i w -> p (i w)"),
                scales[:].rearrange("p i w -> p (i w)"),
                v_with_probs[b][:].rearrange("p i n -> p (i n)"),
            )
            prob_codes[pair], prob_scales[pair] = codes[:, 0], scales[:, 0]
            v_codes[b], v_scales[b] = codes[:, 1], scales[:, 1]

        def quantise_probs(pair, first=0, heads=H):
            if pair not in prob_codes:
                prob_codes[pair] = work.tile([P, WORDS], U32, name="prob_codes", align_bytes=64)[:]
                prob_scales[pair] = work.tile([P, WORDS], U8, name="prob_scales", align_bytes=64)[:]
            words = slice(first * WORDS // H, (first + heads) * WORDS // H)
            quantise(
                prob_codes[pair][:, words],
                prob_scales[pair][:, words],
                probs_grouped[pair][:, first : first + heads].rearrange("p h n -> p (h n)"),
            )

        def product_bank(pair, spare_bank=False):
            if spare_bank:
                products[pair] = score_banks.tile([P, H, D], F32, name="spare_out_bank", tag="score_bank")
            else:
                products[pair] = out_banks.tile([P, H, D], F32, name="out_bank")

        def weighted_values(pair, heads=range(H)):
            b = pair // QT
            for h in heads:
                for g in range(PASSES):
                    first = (h * PASSES + g) * P
                    queries = slice(first, first + P)
                    columns = slice(g * D, (g + 1) * D)
                    nc.tensor.matmul_mx(
                        out=products[pair][:, h, :],
                        lhsT=prob_codes[pair][:, queries].bitcast(FP8X4),
                        lhsT_scale=prob_scales[pair][:, queries],
                        rhs=v_codes[b][:, columns].bitcast(FP8X4),
                        rhs_scale=v_scales[b][:, columns],
                        start=(g == 0),
                        stop=(g == PASSES - 1),
                    )

        def normalise(pair, h, on_vector=False):
            if pair not in result:
                result[pair] = result_pool.tile([P, H, D], F32, name="result")
            factor = inv_sum[pair][:, h : h + 1]
            if on_vector:
                nc.vector.tensor_scalar_mul(out=result[pair][:, h, :], in0=products[pair][:, h, :], scalar1=factor)
            else:
                nc.scalar.activation(
                    out=result[pair][:, h, :], in_=products[pair][:, h, :], func=ACT.Copy, scale=factor
                )

        def store(pair):
            b, qt = divmod(pair, QT)
            nc.sync.dma_start(out=out[b, qt * P : (qt + 1) * P, :, :], in_=result[pair][:])

        def normalise_and_store(pair, on_vector=False):
            for h in range(H):
                normalise(pair, h, on_vector)
            store(pair)

        flip_keys(0, 0, operand_bank(idle_score_bank=True))
        flip_keys(0, 1, operand_bank(idle_score_bank=True), copy=nc.vector.tensor_copy)
        flip_queries(0, operand_bank(idle_score_bank=True))
        flip_keys(0, 2, operand_bank(idle_score_bank=True), copy=nc.vector.tensor_copy)
        flip_keys(0, 3, operand_bank())

        score_matmuls(0, [0])
        flip_queries(1, operand_bank())
        score_matmuls(0, [1])
        weigh(0, [0])
        add_bias_to_head(0, 0, nc.gpsimd)
        weigh(0, [1])
        score_matmuls(1)
        bank = operand_bank()
        for i in range(2):
            transpose_queries(2 + i, bank[:, i])
        for i in range(2):
            copy_queries(2 + i, bank[:, i])
        weigh(1, [0])
        add_bias_to_head(0, 1, nc.vector)
        for h in range(H):
            row_maxima(0, h)
        add_bias_to_head(1, 0, nc.gpsimd)
        weigh(1, [1])
        add_bias_to_head(1, 1, nc.gpsimd)
        score_matmuls(2)
        for h in range(H):
            exponentials(0, h)
        for piece in range(VALUE_PIECES):
            group_values(0, piece)
        weigh(2)
        score_matmuls(3)
        flip_operands(0)
        for h in range(H):
            flip_probs(0, h)

        last = PAIRS - 1
        for step in range(1, last - 1):
            row_maxima(step, 0)
            exponentials(step, 0)
            group_probs(step - 1)
            weigh(step + 2, [0])
            if live(step + SCORE_LEAD):
                score_matmuls(step + SCORE_LEAD, [0])
            flip_probs(step, 0)
            row_maxima(step, 1)
            exponentials(step, 1)
            if live(step - 3):
                normalise_and_store(step - 3)
            if step % 2 == 0:
                invert_sums(step - 2, pairs=2)
            weigh(step + 2, [1])
            flip_operands(step)
            if live(step + SCORE_LEAD):
                score_matmuls(step + SCORE_LEAD, [1])
            flip_probs(step, 1)
            if step % QT >= KEY_QUARTERS and step // QT + 1 < B:
                group_values(step // QT + 1, step % QT - KEY_QUARTERS)
            add_bias(step + 1)
            if live(step - 2):
                if (step - 2) % QT == 0:
                    quantise_probs_and_values(step - 2)
                else:
                    quantise_probs(step - 2)
            if live(step - 2):
                product_bank(step - 2)
                weighted_values(step - 2)

        for h in reversed(range(H)):
            add_bias_to_head(last, h, nc.gpsimd)
        for h in range(H):
            row_maxima(last - 1, h)
        group_probs(last - 2)
        for h in range(H):
            exponentials(last - 1, h)
            flip_probs(last - 1, h)
        invert_sums(last - 3, pairs=2)
        row_maxima(last, 1)
        normalise_and_store(last - 4, on_vector=True)
        row_maxima(last, 0)
        exponentials(last, 1)
        flip_probs(last, 1, spare_bank=True)
        exponentials(last, 0)
        quantise_probs(last - 3)
        product_bank(last - 3)
        weighted_values(last - 3)
        flip_probs(last, 0, spare_bank=True)
        quantise_probs(last - 2)
        product_bank(last - 2, spare_bank=True)
        weighted_values(last - 2)
        invert_sums(last - 1)
        group_probs(last - 1, copy=nc.vector.tensor_copy)
        group_probs(last, heads=[1])
        normalise_and_store(last - 3)
        group_probs(last, heads=[0])
        quantise_probs(last - 1)
        product_bank(last - 1, spare_bank=True)
        weighted_values(last - 1)
        normalise_and_store(last - 2)
        invert_sums(last)
        product_bank(last)
        for h in reversed(range(H)):
            quantise_probs(last, h, 1)
            weighted_values(last, [h])
        normalise_and_store(last - 1)
        normalise(last, 1)
        normalise(last, 0, on_vector=True)
        store(last)
